import numpy as np
import ml_dtypes


def mxq(x, axis, fmt="e4m3"):
    dtype, down = {"e4m3": (ml_dtypes.float8_e4m3fn, 7), "e5m2": (ml_dtypes.float8_e5m2, 14)}[fmt]
    v = np.moveaxis(np.asarray(x, np.float32).astype(ml_dtypes.bfloat16).astype(np.float64), axis, -1)
    blocks = v.reshape(v.shape[:-1] + (-1, 32))
    amax = np.abs(blocks).max(-1, keepdims=True)
    byte = np.maximum(np.where(amax > 0, np.frexp(amax)[1] - 1 + 127, 0) - down, 1)
    scale = np.exp2(byte - 127.0)
    codes = (blocks / scale).astype(np.float32).astype(dtype).astype(np.float64)
    return np.moveaxis((codes * scale).reshape(v.shape), -1, axis)


WIDE = False


def mx_kscale(k):
    if not WIDE:
        return np.ones(k)
    levels = np.array([10, -10, 5, -5, 0])
    a = np.random.permutation(np.resize(levels, k // 512 * 4)).reshape(k // 512, 4)
    idx = np.arange(k)
    return np.exp2(a[idx // 512, idx % 128 // 32])


BF16 = ml_dtypes.bfloat16


def bf(x):
    return np.asarray(x, np.float32).astype(BF16)


def f64(x):
    return np.asarray(x).astype(np.float64)


E2M1 = np.array([0.0, 0.5, 1.0, 1.5, 2.0, 3.0, 4.0, 6.0, -0.0, -0.5, -1.0, -1.5, -2.0, -3.0, -4.0, -6.0])


def pack_weight(w, fmt):
    k, n = w.shape
    w = f64(bf(w)).reshape(k // 32, 32, n)
    amax = np.abs(w).max(1)
    if fmt == "e4m3":
        byte = np.frexp(amax)[1] - 1 + 127 - 7
    else:
        mant, ex = np.frexp(amax / 6.0)
        byte = np.where(mant > 0.5, ex, ex - 1) + 127
    byte = np.clip(np.where(amax > 0, byte, 1), 1, 254)
    scaled = (w * np.exp2(127.0 - byte)[:, None, :]).reshape(k, n).astype(np.float32)
    by_word = np.ascontiguousarray(scaled.reshape(k // 512, 128, 4, n).transpose(0, 1, 3, 2))
    if fmt == "e4m3":
        words = by_word.astype(ml_dtypes.float8_e4m3fn).view(np.uint8)
    else:
        c = by_word.astype(ml_dtypes.float4_e2m1fn).view(np.uint8) & 0xF
        words = c[..., 0::2] | (c[..., 1::2] << 4)
    return np.ascontiguousarray(words), np.ascontiguousarray(byte.astype(np.uint8).reshape(k // 512, 16, n))


def unpack_weight(words, scales, fmt):
    g, p, n, _ = words.shape
    if fmt == "e4m3":
        vals = np.ascontiguousarray(words).view(ml_dtypes.float8_e4m3fn).astype(np.float64)
    else:
        nib = np.empty((g, p, n, 4), np.uint8)
        nib[..., 0::2] = words & 0xF
        nib[..., 1::2] = words >> 4
        vals = E2M1[nib]
    vals = vals * np.repeat(np.exp2(scales.astype(np.float64) - 127.0), 8, axis=1)[..., None]
    return vals.transpose(0, 1, 3, 2).reshape(g * 512, n)


B, N, D, H, Z = 8, 512, 1024, 1, 512
NEG_INF = -1.0e9
CW = 1.3 / Z ** 0.25
FMT = "e4m3"


def setup_inputs():
    s, t = mx_kscale(D), mx_kscale(Z)
    g1 = np.random.standard_normal((H, Z, D))
    g2 = np.random.standard_normal((H, Z, D))
    x = bf(np.random.standard_normal((B, N, D)) * s)
    wk = (0.25 * g1 + g2) * CW / np.sqrt(D) / s / t[None, :, None]
    wq = g1 * CW / np.sqrt(D) / s * t[None, :, None]
    wk_words, wk_scales = pack_weight(wk.swapaxes(1, 2).reshape(-1, Z), FMT)
    wq_words, wq_scales = pack_weight(wq.swapaxes(1, 2).reshape(-1, Z), FMT)
    betas = bf(1.5 + 0.15 * np.random.standard_normal(H))
    return {"x": x,
            "wk_words": wk_words, "wk_scales": wk_scales,
            "wq_words": wq_words, "wq_scales": wq_scales,
            "betas": betas}


def reference(x, wk_words, wk_scales, wq_words, wq_scales, betas):
    beta = f64(betas)
    xq = mxq(f64(x).reshape(B * N, D), 1, "e4m3")
    k = (xq @ unpack_weight(wk_words, wk_scales, FMT).reshape(H, D, Z).swapaxes(1, 2).reshape(H * Z, D).T).reshape(B, N, H, Z).transpose(0, 2, 1, 3)
    q = (xq @ unpack_weight(wq_words, wq_scales, FMT).reshape(H, D, Z).swapaxes(1, 2).reshape(H * Z, D).T).reshape(B, N, H, Z).transpose(0, 2, 1, 3)
    a = beta[None, :, None, None] * (mxq(q, 3, "e4m3") @ mxq(k, 3, "e4m3").transpose(0, 1, 3, 2))
    a = np.where(np.eye(N, dtype=bool)[None, None], NEG_INF, a)
    top = a.max(-1, keepdims=True)
    lse = top[..., 0] + np.log(np.exp(a - top).sum(-1))
    return -(lse / beta[None, :, None])

@@ -1,0 +1,238 @@
+from contextlib import ExitStack
+
+import concourse.masks as masks
+import concourse.mybir as mybir
+
+F32 = mybir.dt.float32
+BF16 = mybir.dt.bfloat16
+I32 = mybir.dt.int32
+U32 = mybir.dt.uint32
+U8 = mybir.dt.uint8
+FP8X4 = mybir.dt.float8_e4m3fn_x4
+ALU = mybir.AluOpType
+ACT = mybir.ActivationFunctionType
+
+P = 128
+PACK = 4
+BATCH = 8
+TOKENS = 512
+FEATURES = 1024
+HEAD = 512
+TILES = TOKENS // P
+PASSES = FEATURES // (P * PACK)
+WORDS = P * PACK // 2
+ROWS = BATCH * TILES
+Q, K = 0, 1
+MASKED = 1.0e9
+BIG = 3.0e38
+
+FLOPS = 2 * BATCH * TOKENS * FEATURES * HEAD * 2 + 2 * BATCH * TOKENS * TOKENS * HEAD
+
+
+def tile_multiheadenergyattention_pa_t_e_kernel(
+    tc, x, wk_words, wk_scales, wq_words, wq_scales, betas, out
+):
+    nc = tc.nc
+    with ExitStack() as stack:
+        keep = stack.enter_context(tc.tile_pool(name="keep", bufs=1))
+        ring = stack.enter_context(tc.tile_pool(name="ring", bufs=2))
+        psum_flip = stack.enter_context(tc.psum_pool(name="psum_flip", bufs=2))
+        psum_proj = stack.enter_context(tc.psum_pool(name="psum_proj", bufs=2))
+        psum_score = stack.enter_context(tc.psum_pool(name="psum_score", bufs=TILES))
+        stack.enter_context(tc.manual_schedule())
+
+        ident = keep.tile([P, P], F32)
+        masks.make_identity(nc, ident[:])
+        w_planes = keep.tile([P, 2, PASSES, HEAD], U8, align_bytes=64)
+        nc.vector.memset(w_planes[:].rearrange("p w g n -> p (w g n)").bitcast(I32), 0)
+        result = keep.tile([P, P], F32)
+        nc.vector.memset(result[:], 0.0)
+
+        x_sb = keep.tile([P, ROWS, FEATURES], BF16)
+        x_rows = x.rearrange("b (t p) d -> p (b t) d", p=P)
+
+        def load_x(b):
+            for row in range(b * TILES, (b + 1) * TILES):
+                nc.sync.dma_start(out=x_sb[:, row, :], in_=x_rows[:, row, :])
+
+        load_x(0)
+        beta_bf = keep.tile([P, 1], BF16)
+        nc.sync.dma_start(out=beta_bf[:], in_=betas.partition_broadcast(P))
+        w_codes = keep.tile([P, 2, PASSES, HEAD], U32, align_bytes=64)
+        given = ((wq_words, wq_scales), (wk_words, wk_scales))
+        for w in (Q, K):
+            for i in range(4):
+                nc.sync.dma_start(
+                    out=w_planes[32 * i : 32 * i + 4, w, :, :].bitcast(I32),
+                    in_=given[w][1][:, 4 * i : 4 * i + 4, :].rearrange("g r n -> r g n").bitcast(I32),
+                )
+        for w in (Q, K):
+            nc.sync.dma_start(
+                out=w_codes[:, w, :, :].bitcast(I32),
+                in_=given[w][0].rearrange("g p n t -> p g (n t)").bitcast(I32),
+            )
+        for b in range(1, BATCH):
+            load_x(b)
+
+        neg_beta = keep.tile([P, 1], F32)
+        nc.vector.tensor_scalar_mul(out=neg_beta[:], in0=beta_bf[:], scalar1=-1.0)
+        neg_inv_beta = keep.tile([P, 1], F32)
+        nc.vector.reciprocal(out=neg_inv_beta[:], in_=neg_beta[:])
+        off_diag = keep.tile([P, P], F32)
+        nc.vector.tensor_scalar(
+            out=off_diag[:], in0=ident[:], scalar1=BIG, scalar2=-BIG, op0=ALU.mult, op1=ALU.add
+        )
+        diag_mask = keep.tile([P, P], F32)
+        nc.vector.scalar_tensor_tensor(
+            out=diag_mask[:], in0=ident[:], scalar=MASKED, in1=off_diag[:], op0=ALU.mult, op1=ALU.add
+        )
+
+        neg_top = keep.tile([P, ROWS], F32)
+        exp_sums = keep.tile([P, ROWS], F32)
+
+        x_grouped, x_codes, x_scales = {}, {}, {}
+        qk_grouped, qk_codes, qk_scales = {}, {}, {}
+        score_banks, neg_scores = {}, {}
+
+        def transpose_x(b):
+            grouped = ring.tile([P, PASSES, TOKENS, PACK], BF16, align_bytes=64, name="x_grouped")
+            grouped_words = grouped[:].bitcast(F32)
+            for t in range(TILES):
+                words = x_sb[:, b * TILES + t, :].bitcast(F32)
+                flipped = psum_flip.tile([P, PASSES, 2, P], F32)
+                for g in range(PASSES):
+                    for u in range(2):
+                        nc.tensor.transpose(
+                            flipped[:, g, u, :], words[:, WORDS * g + u : WORDS * (g + 1) : 2], ident[:]
+                        )
+                nc.vector.tensor_copy(
+                    out=grouped_words[:, :, t * P : (t + 1) * P, :],
+                    in_=flipped[:].rearrange("p g u r -> p g r u"),
+                )
+            x_grouped[b] = grouped
+
+        def quantise(grouped, what):
+            codes = ring.tile([P, 2, TOKENS], U32, align_bytes=64, name=what + "_codes")
+            scales = ring.tile([P, 2, TOKENS], U8, align_bytes=64, name=what + "_scales")
+            nc.vector.quantize_mx(
+                out=codes[:].rearrange("p a r -> p (a r)").bitcast(FP8X4),
+                scales=scales[:].rearrange("p a r -> p (a r)"),
+                in_=grouped[:].rearrange("p a r t -> p (a r t)"),
+            )
+            return codes, scales
+
+        def quantise_x(b):
+            x_codes[b], x_scales[b] = quantise(x_grouped[b], "x")
+
+        def project(b):
+            grouped = ring.tile([P, 2, TOKENS, PACK], BF16, align_bytes=64, name="qk_grouped")
+            for t in range(TILES):
+                tokens = slice(t * P, (t + 1) * P)
+                for w in (Q, K):
+                    bank = psum_proj.tile([P, PACK, P], F32)
+                    for z in range(PACK):
+                        heads = slice(z * P, (z + 1) * P)
+                        for g in range(PASSES):
+                            nc.tensor.matmul_mx(
+                                out=bank[:, z, :],
+                                lhsT=w_codes[:, w, g, heads].bitcast(FP8X4),
+                                lhsT_scale=w_planes[:, w, g, heads],
+                                rhs=x_codes[b][:, g, tokens].bitcast(FP8X4),
+                                rhs_scale=x_scales[b][:, g, tokens],
+                                start=(g == 0),
+                                stop=(g == PASSES - 1),
+                            )
+                    nc.scalar.copy(out=grouped[:, w, tokens, :], in_=bank[:].rearrange("p z r -> p r z"))
+            qk_grouped[b] = grouped
+
+        def quantise_qk(b):
+            qk_codes[b], qk_scales[b] = quantise(qk_grouped[b], "qk")
+
+        def scores(b):
+            score_banks[b] = []
+            for n in range(TILES):
+                queries = slice(n * P, (n + 1) * P)
+                bank = psum_score.tile([P, TILES, P], F32)
+                for j in range(TILES):
+                    m = (n + j) % TILES
+                    keys = slice(m * P, (m + 1) * P)
+                    nc.tensor.matmul_mx(
+                        out=bank[:, j, :],
+                        lhsT=qk_codes[b][:, Q, queries].bitcast(FP8X4),
+                        lhsT_scale=qk_scales[b][:, Q, queries],
+                        rhs=qk_codes[b][:, K, keys].bitcast(FP8X4),
+                        rhs_scale=qk_scales[b][:, K, keys],
+                        start=True,
+                        stop=True,
+                    )
+                score_banks[b].append(bank)
+
+        def mask_and_max(b):
+            neg = ring.tile([P, TILES, TOKENS], F32)
+            diag_min = ring.tile([P, TILES], F32)
+            for n in range(TILES):
+                nc.vector.scalar_tensor_tensor(
+                    out=neg[:, n, 0:P],
+                    in0=score_banks[b][n][:, 0, :],
+                    scalar=neg_beta[:, 0:1],
+                    in1=diag_mask[:],
+                    op0=ALU.mult,
+                    op1=ALU.max,
+                )
+            nc.vector.tensor_reduce(
+                out=diag_min[:], in_=neg[:, :, 0:P], axis=mybir.AxisListType.X, op=ALU.min
+            )
+            for n in range(TILES):
+                nc.vector.tensor_scalar(
+                    out=neg[:, n, P:TOKENS],
+                    in0=score_banks[b][n][:, 1:TILES, :].rearrange("p j r -> p (j r)"),
+                    scalar1=neg_beta[:, 0:1],
+                    scalar2=diag_min[:, n : n + 1],
+                    op0=ALU.mult,
+                    op1=ALU.min,
+                    accum_out=neg_top[:, b * TILES + n : b * TILES + n + 1],
+                )
+            neg_scores[b] = neg
+
+        def exp_sum(b):
+            for n in range(TILES):
+                row = b * TILES + n
+                nc.scalar.activation(
+                    out=neg_scores[b][:, n, :],
+                    in_=neg_scores[b][:, n, :],
+                    func=ACT.Exp,
+                    bias=neg_top[:, row : row + 1],
+                    scale=-1.0,
+                    accum_out=exp_sums[:, row : row + 1],
+                )
+
+        def run(stage, b):
+            if 0 <= b < BATCH:
+                stage(b)
+
+        for step in range(BATCH + 4):
+            run(exp_sum, step - 4)
+            run(transpose_x, step)
+            run(quantise_qk, step - 2)
+            run(project, step - 1)
+            run(mask_and_max, step - 3)
+            run(scores, step - 2)
+            run(quantise_x, step)
+
+        ln_sums = keep.tile([P, ROWS], F32)
+        nc.scalar.activation(out=ln_sums[:], in_=exp_sums[:], func=ACT.Ln)
+        top_over_beta = keep.tile([P, ROWS], F32)
+        nc.vector.tensor_scalar_mul(out=top_over_beta[:], in0=neg_top[:], scalar1=neg_inv_beta[:, 0:1])
+        nc.vector.scalar_tensor_tensor(
+            out=result[:, 0:ROWS],
+            in0=ln_sums[:],
+            scalar=neg_inv_beta[:, 0:1],
+            in1=top_over_beta[:],
+            op0=ALU.mult,
+            op1=ALU.subtract,
+        )
+        flipped = psum_flip.tile([P, PASSES, 2, P], F32)
+        nc.tensor.transpose(flipped[:, 0, 0, :], result[:], ident[:])
+        out_rows = keep.tile([ROWS, P], F32)
+        nc.vector.tensor_copy(out=out_rows[:], in_=flipped[0:ROWS, 0, 0, :])
+        nc.sync.dma_start(out=out.rearrange("b h (t p) -> (b h t) p", p=P), in_=out_rows[:])

@@ -22,6 +22,7 @@ TILES = TOKENS // P
 PASSES = FEATURES // (P * PACK)
 WORDS = P * PACK // 2
 ROWS = BATCH * TILES
+BANKS = 8
 Q, K = 0, 1
 MASKED = 1.0e9
 BIG = 3.0e38
@@ -36,17 +37,20 @@ def tile_multiheadenergyattention_pa_t_e_kernel(
     with ExitStack() as stack:
         keep = stack.enter_context(tc.tile_pool(name="keep", bufs=1))
         ring = stack.enter_context(tc.tile_pool(name="ring", bufs=2))
-        psum_flip = stack.enter_context(tc.psum_pool(name="psum_flip", bufs=2))
-        psum_proj = stack.enter_context(tc.psum_pool(name="psum_proj", bufs=2))
-        psum_score = stack.enter_context(tc.psum_pool(name="psum_score", bufs=TILES))
+        pairs = stack.enter_context(tc.tile_pool(name="pairs", bufs=4))
+        psum = stack.enter_context(tc.psum_pool(name="psum", bufs=BANKS))
         stack.enter_context(tc.manual_schedule())
 
+        beta_bf = keep.tile([P, 1], BF16)
+        nc.sync.dma_start(out=beta_bf[:], in_=betas.partition_broadcast(P))
         ident = keep.tile([P, P], F32)
         masks.make_identity(nc, ident[:])
         w_planes = keep.tile([P, 2, PASSES, HEAD], U8, align_bytes=64)
         nc.vector.memset(w_planes[:].rearrange("p w g n -> p (w g n)").bitcast(I32), 0)
         result = keep.tile([P, P], F32)
         nc.vector.memset(result[:], 0.0)
+        warm = keep.tile([P, 1], F32)
+        nc.scalar.activation(out=warm[:], in_=result[:, 0:1], func=ACT.Exp)
 
         x_sb = keep.tile([P, ROWS, FEATURES], BF16)
         x_rows = x.rearrange("b (t p) d -> p (b t) d", p=P)
@@ -56,8 +60,7 @@ def tile_multiheadenergyattention_pa_t_e_kernel(
                 nc.sync.dma_start(out=x_sb[:, row, :], in_=x_rows[:, row, :])
 
         load_x(0)
-        beta_bf = keep.tile([P, 1], BF16)
-        nc.sync.dma_start(out=beta_bf[:], in_=betas.partition_broadcast(P))
+        load_x(1)
         w_codes = keep.tile([P, 2, PASSES, HEAD], U32, align_bytes=64)
         given = ((wq_words, wq_scales), (wk_words, wk_scales))
         for w in (Q, K):
@@ -71,7 +74,7 @@ def tile_multiheadenergyattention_pa_t_e_kernel(
                 out=w_codes[:, w, :, :].bitcast(I32),
                 in_=given[w][0].rearrange("g p n t -> p g (n t)").bitcast(I32),
             )
-        for b in range(1, BATCH):
+        for b in range(2, BATCH):
             load_x(b)
 
         neg_beta = keep.tile([P, 1], F32)
@@ -92,23 +95,27 @@ def tile_multiheadenergyattention_pa_t_e_kernel(
 
         x_grouped, x_codes, x_scales = {}, {}, {}
         qk_grouped, qk_codes, qk_scales = {}, {}, {}
-        score_banks, neg_scores = {}, {}
+        score_bank, neg_scores = {}, {}
+
 
         def transpose_x(b):
+            if not 0 <= b < BATCH:
+                return
             grouped = ring.tile([P, PASSES, TOKENS, PACK], BF16, align_bytes=64, name="x_grouped")
             grouped_words = grouped[:].bitcast(F32)
             for t in range(TILES):
                 words = x_sb[:, b * TILES + t, :].bitcast(F32)
-                flipped = psum_flip.tile([P, PASSES, 2, P], F32)
+                bank = psum.tile([P, 2 * PASSES, P], F32, name="bank")
                 for g in range(PASSES):
                     for u in range(2):
                         nc.tensor.transpose(
-                            flipped[:, g, u, :], words[:, WORDS * g + u : WORDS * (g + 1) : 2], ident[:]
+                            bank[:, 2 * g + u, :], words[:, WORDS * g + u : WORDS * (g + 1) : 2], ident[:]
                         )
-                nc.vector.tensor_copy(
-                    out=grouped_words[:, :, t * P : (t + 1) * P, :],
-                    in_=flipped[:].rearrange("p g u r -> p g r u"),
-                )
+                planes = bank[:].rearrange("p (g u) r -> p g r u", u=2)
+                if t < TILES - 1:
+                    nc.vector.tensor_copy(out=grouped_words[:, :, t * P : (t + 1) * P, :], in_=planes)
+                else:
+                    nc.scalar.copy(out=grouped_words[:, :, t * P : (t + 1) * P, :], in_=planes)
             x_grouped[b] = grouped
 
         def quantise(grouped, what):
@@ -122,58 +129,64 @@ def tile_multiheadenergyattention_pa_t_e_kernel(
             return codes, scales
 
         def quantise_x(b):
-            x_codes[b], x_scales[b] = quantise(x_grouped[b], "x")
+            if 0 <= b < BATCH:
+                x_codes[b], x_scales[b] = quantise(x_grouped[b], "x")
 
-        def project(b):
-            grouped = ring.tile([P, 2, TOKENS, PACK], BF16, align_bytes=64, name="qk_grouped")
-            for t in range(TILES):
-                tokens = slice(t * P, (t + 1) * P)
-                for w in (Q, K):
-                    bank = psum_proj.tile([P, PACK, P], F32)
-                    for z in range(PACK):
-                        heads = slice(z * P, (z + 1) * P)
-                        for g in range(PASSES):
-                            nc.tensor.matmul_mx(
-                                out=bank[:, z, :],
-                                lhsT=w_codes[:, w, g, heads].bitcast(FP8X4),
-                                lhsT_scale=w_planes[:, w, g, heads],
-                                rhs=x_codes[b][:, g, tokens].bitcast(FP8X4),
-                                rhs_scale=x_scales[b][:, g, tokens],
-                                start=(g == 0),
-                                stop=(g == PASSES - 1),
-                            )
-                    nc.scalar.copy(out=grouped[:, w, tokens, :], in_=bank[:].rearrange("p z r -> p r z"))
-            qk_grouped[b] = grouped
+        def project(b, t):
+            if not 0 <= b < BATCH:
+                return
+            if t == 0:
+                qk_grouped[b] = ring.tile([P, 2, TOKENS, PACK], BF16, align_bytes=64, name="qk_grouped")
+            tokens = slice(t * P, (t + 1) * P)
+            for w in (Q, K):
+                bank = psum.tile([P, PACK, P], F32, name="bank")
+                for z in range(PACK):
+                    heads = slice(z * P, (z + 1) * P)
+                    for g in range(PASSES):
+                        nc.tensor.matmul_mx(
+                            out=bank[:, z, :],
+                            lhsT=w_codes[:, w, g, heads].bitcast(FP8X4),
+                            lhsT_scale=w_planes[:, w, g, heads],
+                            rhs=x_codes[b][:, g, tokens].bitcast(FP8X4),
+                            rhs_scale=x_scales[b][:, g, tokens],
+                            start=(g == 0),
+                            stop=(g == PASSES - 1),
+                        )
+                nc.scalar.copy(out=qk_grouped[b][:, w, tokens, :], in_=bank[:].rearrange("p z r -> p r z"))
 
         def quantise_qk(b):
-            qk_codes[b], qk_scales[b] = quantise(qk_grouped[b], "qk")
+            if 0 <= b < BATCH:
+                qk_codes[b], qk_scales[b] = quantise(qk_grouped[b], "qk")
 
-        def scores(b):
-            score_banks[b] = []
-            for n in range(TILES):
-                queries = slice(n * P, (n + 1) * P)
-                bank = psum_score.tile([P, TILES, P], F32)
-                for j in range(TILES):
-                    m = (n + j) % TILES
-                    keys = slice(m * P, (m + 1) * P)
-                    nc.tensor.matmul_mx(
-                        out=bank[:, j, :],
-                        lhsT=qk_codes[b][:, Q, queries].bitcast(FP8X4),
-                        lhsT_scale=qk_scales[b][:, Q, queries],
-                        rhs=qk_codes[b][:, K, keys].bitcast(FP8X4),
-                        rhs_scale=qk_scales[b][:, K, keys],
-                        start=True,
-                        stop=True,
-                    )
-                score_banks[b].append(bank)
+        def scores(row):
+            if not 0 <= row < ROWS:
+                return
+            b, n = divmod(row, TILES)
+            queries = slice(n * P, (n + 1) * P)
+            bank = psum.tile([P, TILES, P], F32, name="bank")
+            for j in range(TILES):
+                m = (n + j) % TILES
+                keys = slice(m * P, (m + 1) * P)
+                nc.tensor.matmul_mx(
+                    out=bank[:, j, :],
+                    lhsT=qk_codes[b][:, Q, queries].bitcast(FP8X4),
+                    lhsT_scale=qk_scales[b][:, Q, queries],
+                    rhs=qk_codes[b][:, K, keys].bitcast(FP8X4),
+                    rhs_scale=qk_scales[b][:, K, keys],
+                    start=True,
+                    stop=True,
+                )
+            score_bank[row] = bank
 
-        def mask_and_max(b):
-            neg = ring.tile([P, TILES, TOKENS], F32)
-            diag_min = ring.tile([P, TILES], F32)
-            for n in range(TILES):
+        def mask_and_max(first):
+            if not 0 <= first < ROWS:
+                return
+            neg = pairs.tile([P, 2, TOKENS], F32, name="neg")
+            diag_min = pairs.tile([P, 2], F32, name="diag_min")
+            for i in range(2):
                 nc.vector.scalar_tensor_tensor(
-                    out=neg[:, n, 0:P],
-                    in0=score_banks[b][n][:, 0, :],
+                    out=neg[:, i, 0:P],
+                    in0=score_bank[first + i][:, 0, :],
                     scalar=neg_beta[:, 0:1],
                     in1=diag_mask[:],
                     op0=ALU.mult,
@@ -182,42 +195,43 @@ def tile_multiheadenergyattention_pa_t_e_kernel(
             nc.vector.tensor_reduce(
                 out=diag_min[:], in_=neg[:, :, 0:P], axis=mybir.AxisListType.X, op=ALU.min
             )
-            for n in range(TILES):
+            for i in range(2):
                 nc.vector.tensor_scalar(
-                    out=neg[:, n, P:TOKENS],
-                    in0=score_banks[b][n][:, 1:TILES, :].rearrange("p j r -> p (j r)"),
+                    out=neg[:, i, P:TOKENS],
+                    in0=score_bank[first + i][:, 1:TILES, :].rearrange("p j r -> p (j r)"),
                     scalar1=neg_beta[:, 0:1],
-                    scalar2=diag_min[:, n : n + 1],
+                    scalar2=diag_min[:, i : i + 1],
                     op0=ALU.mult,
                     op1=ALU.min,
-                    accum_out=neg_top[:, b * TILES + n : b * TILES + n + 1],
+                    accum_out=neg_top[:, first + i : first + i + 1],
                 )
-            neg_scores[b] = neg
+                neg_scores[first + i] = neg[:, i, :]
 
-        def exp_sum(b):
-            for n in range(TILES):
-                row = b * TILES + n
-                nc.scalar.activation(
-                    out=neg_scores[b][:, n, :],
-                    in_=neg_scores[b][:, n, :],
-                    func=ACT.Exp,
-                    bias=neg_top[:, row : row + 1],
-                    scale=-1.0,
-                    accum_out=exp_sums[:, row : row + 1],
-                )
+        def exp_sum(row):
+            if not 0 <= row < ROWS:
+                return
+            nc.scalar.activation(
+                out=neg_scores[row],
+                in_=neg_scores[row],
+                func=ACT.Exp,
+                bias=neg_top[:, row : row + 1],
+                scale=-1.0,
+                accum_out=exp_sums[:, row : row + 1],
+            )
 
-        def run(stage, b):
-            if 0 <= b < BATCH:
-                stage(b)
-
-        for step in range(BATCH + 4):
-            run(exp_sum, step - 4)
-            run(transpose_x, step)
-            run(quantise_qk, step - 2)
-            run(project, step - 1)
-            run(mask_and_max, step - 3)
-            run(scores, step - 2)
-            run(quantise_x, step)
+        for step in range(BATCH + 5):
+            for half in range(2):
+                if half == 0:
+                    quantise_x(step - 1)
+                else:
+                    quantise_qk(step - 3)
+                first = (step - 4) * TILES + 2 * half
+                for row in (first, first + 1):
+                    project(step - 2, row % TILES)
+                    scores(row)
+                    exp_sum(row - 2)
+                mask_and_max(first)
+            transpose_x(step)
 
         ln_sums = keep.tile([P, ROWS], F32)
         nc.scalar.activation(out=ln_sums[:], in_=exp_sums[:], func=ACT.Ln)
@@ -231,8 +245,8 @@ def tile_multiheadenergyattention_pa_t_e_kernel(
             op0=ALU.mult,
             op1=ALU.subtract,
         )
-        flipped = psum_flip.tile([P, PASSES, 2, P], F32)
-        nc.tensor.transpose(flipped[:, 0, 0, :], result[:], ident[:])
+        bank = psum.tile([P, PACK, P], F32, name="bank")
+        nc.tensor.transpose(bank[:, 0, :], result[:], ident[:])
         out_rows = keep.tile([ROWS, P], F32)
-        nc.vector.tensor_copy(out=out_rows[:], in_=flipped[0:ROWS, 0, 0, :])
+        nc.vector.tensor_copy(out=out_rows[:], in_=bank[0:ROWS, 0, :])
         nc.sync.dma_start(out=out.rearrange("b h (t p) -> (b h t) p", p=P), in_=out_rows[:])

@@ -63,13 +63,13 @@ def tile_multiheadenergyattention_pa_t_e_kernel(
         load_x(1)
         w_codes = keep.tile([P, 2, PASSES, HEAD], U32, align_bytes=64)
         given = ((wq_words, wq_scales), (wk_words, wk_scales))
-        for w in (Q, K):
+        for w in (K, Q):
             for i in range(4):
                 nc.sync.dma_start(
                     out=w_planes[32 * i : 32 * i + 4, w, :, :].bitcast(I32),
                     in_=given[w][1][:, 4 * i : 4 * i + 4, :].rearrange("g r n -> r g n").bitcast(I32),
                 )
-        for w in (Q, K):
+        for w in (K, Q):
             nc.sync.dma_start(
                 out=w_codes[:, w, :, :].bitcast(I32),
                 in_=given[w][0].rearrange("g p n t -> p g (n t)").bitcast(I32),
@@ -95,7 +95,7 @@ def tile_multiheadenergyattention_pa_t_e_kernel(
 
         x_grouped, x_codes, x_scales = {}, {}, {}
         qk_grouped, qk_codes, qk_scales = {}, {}, {}
-        score_bank, neg_scores = {}, {}
+        score_bank, neg_scores, diag_min, rest_min = {}, {}, {}, {}
 
 
         def transpose_x(b):
@@ -118,45 +118,44 @@ def tile_multiheadenergyattention_pa_t_e_kernel(
                     nc.scalar.copy(out=grouped_words[:, :, t * P : (t + 1) * P, :], in_=planes)
             x_grouped[b] = grouped
 
-        def quantise(grouped, what):
-            codes = ring.tile([P, 2, TOKENS], U32, align_bytes=64, name=what + "_codes")
-            scales = ring.tile([P, 2, TOKENS], U8, align_bytes=64, name=what + "_scales")
-            nc.vector.quantize_mx(
-                out=codes[:].rearrange("p a r -> p (a r)").bitcast(FP8X4),
-                scales=scales[:].rearrange("p a r -> p (a r)"),
-                in_=grouped[:].rearrange("p a r t -> p (a r t)"),
-            )
-            return codes, scales
-
         def quantise_x(b):
-            if 0 <= b < BATCH:
-                x_codes[b], x_scales[b] = quantise(x_grouped[b], "x")
-
-        def project(b, t):
             if not 0 <= b < BATCH:
                 return
-            if t == 0:
-                qk_grouped[b] = ring.tile([P, 2, TOKENS, PACK], BF16, align_bytes=64, name="qk_grouped")
-            tokens = slice(t * P, (t + 1) * P)
-            for w in (Q, K):
-                bank = psum.tile([P, PACK, P], F32, name="bank")
-                for z in range(PACK):
-                    heads = slice(z * P, (z + 1) * P)
-                    for g in range(PASSES):
-                        nc.tensor.matmul_mx(
-                            out=bank[:, z, :],
-                            lhsT=w_codes[:, w, g, heads].bitcast(FP8X4),
-                            lhsT_scale=w_planes[:, w, g, heads],
-                            rhs=x_codes[b][:, g, tokens].bitcast(FP8X4),
-                            rhs_scale=x_scales[b][:, g, tokens],
-                            start=(g == 0),
-                            stop=(g == PASSES - 1),
-                        )
-                nc.scalar.copy(out=qk_grouped[b][:, w, tokens, :], in_=bank[:].rearrange("p z r -> p r z"))
+            x_codes[b] = ring.tile([P, PASSES, TOKENS], U32, align_bytes=64, name="x_codes")
+            x_scales[b] = ring.tile([P, PASSES, TOKENS], U8, align_bytes=64, name="x_scales")
+            nc.vector.quantize_mx(
+                out=x_codes[b][:].rearrange("p g r -> p (g r)").bitcast(FP8X4),
+                scales=x_scales[b][:].rearrange("p g r -> p (g r)"),
+                in_=x_grouped[b][:].rearrange("p g r t -> p (g r t)"),
+            )
 
-        def quantise_qk(b):
-            if 0 <= b < BATCH:
-                qk_codes[b], qk_scales[b] = quantise(qk_grouped[b], "qk")
+        def project(b, w, t):
+            if not 0 <= b < BATCH:
+                return
+            tokens = slice(t * P, (t + 1) * P)
+            bank = psum.tile([P, PACK, P], F32, name="bank")
+            for z in range(PACK):
+                heads = slice(z * P, (z + 1) * P)
+                for g in range(PASSES):
+                    nc.tensor.matmul_mx(
+                        out=bank[:, z, :],
+                        lhsT=w_codes[:, w, g, heads].bitcast(FP8X4),
+                        lhsT_scale=w_planes[:, w, g, heads],
+                        rhs=x_codes[b][:, g, tokens].bitcast(FP8X4),
+                        rhs_scale=x_scales[b][:, g, tokens],
+                        start=(g == 0),
+                        stop=(g == PASSES - 1),
+                    )
+            nc.scalar.copy(out=qk_grouped[b][:, w, tokens, :], in_=bank[:].rearrange("p z r -> p r z"))
+
+        def quantise_qk(b, w, tokens):
+            if not 0 <= b < BATCH:
+                return
+            nc.vector.quantize_mx(
+                out=qk_codes[b][:, w, tokens].bitcast(FP8X4),
+                scales=qk_scales[b][:, w, tokens],
+                in_=qk_grouped[b][:, w, tokens, :].rearrange("p r t -> p (r t)"),
+            )
 
         def scores(row):
             if not 0 <= row < ROWS:
@@ -178,11 +177,12 @@ def tile_multiheadenergyattention_pa_t_e_kernel(
                 )
             score_bank[row] = bank
 
-        def mask_and_max(first):
+        def mask_and_min(first):
             if not 0 <= first < ROWS:
                 return
             neg = pairs.tile([P, 2, TOKENS], F32, name="neg")
-            diag_min = pairs.tile([P, 2], F32, name="diag_min")
+            diag_min[first] = pairs.tile([P, 2], F32, name="diag_min")
+            rest_min[first] = pairs.tile([P, 2], F32, name="rest_min")
             for i in range(2):
                 nc.vector.scalar_tensor_tensor(
                     out=neg[:, i, 0:P],
@@ -192,20 +192,27 @@ def tile_multiheadenergyattention_pa_t_e_kernel(
                     op0=ALU.mult,
                     op1=ALU.max,
                 )
-            nc.vector.tensor_reduce(
-                out=diag_min[:], in_=neg[:, :, 0:P], axis=mybir.AxisListType.X, op=ALU.min
-            )
             for i in range(2):
                 nc.vector.tensor_scalar(
                     out=neg[:, i, P:TOKENS],
                     in0=score_bank[first + i][:, 1:TILES, :].rearrange("p j r -> p (j r)"),
                     scalar1=neg_beta[:, 0:1],
-                    scalar2=diag_min[:, i : i + 1],
+                    scalar2=None,
                     op0=ALU.mult,
                     op1=ALU.min,
-                    accum_out=neg_top[:, first + i : first + i + 1],
+                    accum_out=rest_min[first][:, i : i + 1],
                 )
                 neg_scores[first + i] = neg[:, i, :]
+            nc.vector.tensor_reduce(
+                out=diag_min[first][:], in_=neg[:, :, 0:P], axis=mybir.AxisListType.X, op=ALU.min
+            )
+
+        def join_min(first):
+            if not 0 <= first < ROWS:
+                return
+            nc.vector.tensor_tensor(
+                out=neg_top[:, first : first + 2], in0=diag_min[first][:], in1=rest_min[first][:], op=ALU.min
+            )
 
         def exp_sum(row):
             if not 0 <= row < ROWS:
@@ -219,18 +226,32 @@ def tile_multiheadenergyattention_pa_t_e_kernel(
                 accum_out=exp_sums[:, row : row + 1],
             )
 
-        for step in range(BATCH + 5):
-            for half in range(2):
-                if half == 0:
-                    quantise_x(step - 1)
-                else:
-                    quantise_qk(step - 3)
-                first = (step - 4) * TILES + 2 * half
-                for row in (first, first + 1):
-                    project(step - 2, row % TILES)
-                    scores(row)
-                    exp_sum(row - 2)
-                mask_and_max(first)
+        def quarter(b, w, t, row):
+            project(b, w, t)
+            project(b, w, t + 1)
+            scores(row)
+            exp_sum(row - 4)
+
+        first_half, second_half = slice(0, TOKENS // 2), slice(TOKENS // 2, TOKENS)
+        for step in range(BATCH + 4):
+            b = step - 2
+            row = (step - 3) * TILES
+            if 0 <= b < BATCH:
+                qk_grouped[b] = ring.tile([P, 2, TOKENS, PACK], BF16, align_bytes=64, name="qk_grouped")
+                qk_codes[b] = ring.tile([P, 2, TOKENS], U32, align_bytes=64, name="qk_codes")
+                qk_scales[b] = ring.tile([P, 2, TOKENS], U8, align_bytes=64, name="qk_scales")
+            quantise_x(step - 1)
+            join_min(row - 2)
+            quarter(b, K, 0, row)
+            quarter(b, K, 2, row + 1)
+            mask_and_min(row)
+            quantise_qk(b, K, slice(0, TOKENS))
+            join_min(row)
+            quarter(b, Q, 0, row + 2)
+            quantise_qk(b, Q, first_half)
+            quarter(b, Q, 2, row + 3)
+            mask_and_min(row + 2)
+            quantise_qk(b, Q, second_half)
             transpose_x(step)
 
         ln_sums = keep.tile([P, ROWS], F32)

@@ -47,10 +47,12 @@ def tile_multiheadenergyattention_pa_t_e_kernel(
         masks.make_identity(nc, ident[:])
         w_planes = keep.tile([P, 2, PASSES, HEAD], U8, align_bytes=64)
         nc.vector.memset(w_planes[:].rearrange("p w g n -> p (w g n)").bitcast(I32), 0)
-        result = keep.tile([P, P], F32)
-        nc.vector.memset(result[:], 0.0)
+        neg_top = keep.tile([P, P], F32)
+        exp_sums = keep.tile([P, P], F32)
+        nc.vector.memset(neg_top[:], 0.0)
+        nc.vector.memset(exp_sums[:], 0.0)
         warm = keep.tile([P, 1], F32)
-        nc.scalar.activation(out=warm[:], in_=result[:, 0:1], func=ACT.Exp)
+        nc.scalar.activation(out=warm[:], in_=neg_top[:, 0:1], func=ACT.Exp)
 
         x_sb = keep.tile([P, ROWS, FEATURES], BF16)
         x_rows = x.rearrange("b (t p) d -> p (b t) d", p=P)
@@ -89,9 +91,6 @@ def tile_multiheadenergyattention_pa_t_e_kernel(
         nc.vector.scalar_tensor_tensor(
             out=diag_mask[:], in0=ident[:], scalar=MASKED, in1=off_diag[:], op0=ALU.mult, op1=ALU.add
         )
-
-        neg_top = keep.tile([P, ROWS], F32)
-        exp_sums = keep.tile([P, ROWS], F32)
 
         x_grouped, x_codes, x_scales = {}, {}, {}
         qk_grouped, qk_codes, qk_scales = {}, {}, {}
@@ -254,20 +253,24 @@ def tile_multiheadenergyattention_pa_t_e_kernel(
             quantise_qk(b, Q, second_half)
             transpose_x(step)
 
-        ln_sums = keep.tile([P, ROWS], F32)
-        nc.scalar.activation(out=ln_sums[:], in_=exp_sums[:], func=ACT.Ln)
-        top_over_beta = keep.tile([P, ROWS], F32)
-        nc.vector.tensor_scalar_mul(out=top_over_beta[:], in0=neg_top[:], scalar1=neg_inv_beta[:, 0:1])
+        nc.scalar.activation(out=warm[:], in_=warm[:], func=ACT.Ln)
+        top_bank = psum.tile([P, PACK, P], F32, name="bank")
+        nc.tensor.transpose(top_bank[:, 0, :], neg_top[:], ident[:])
+        top_over_beta = keep.tile([ROWS, P], F32)
+        nc.vector.tensor_scalar_mul(
+            out=top_over_beta[:], in0=top_bank[0:ROWS, 0, :], scalar1=neg_inv_beta[0:ROWS, 0:1]
+        )
+        sum_bank = psum.tile([P, PACK, P], F32, name="bank")
+        nc.tensor.transpose(sum_bank[:, 0, :], exp_sums[:], ident[:])
+        ln_sums = keep.tile([ROWS, P], F32)
+        nc.scalar.activation(out=ln_sums[:], in_=sum_bank[0:ROWS, 0, :], func=ACT.Ln)
+        out_rows = keep.tile([ROWS, P], F32)
         nc.vector.scalar_tensor_tensor(
-            out=result[:, 0:ROWS],
+            out=out_rows[:],
             in0=ln_sums[:],
-            scalar=neg_inv_beta[:, 0:1],
+            scalar=neg_inv_beta[0:ROWS, 0:1],
             in1=top_over_beta[:],
             op0=ALU.mult,
             op1=ALU.subtract,
         )
-        bank = psum.tile([P, PACK, P], F32, name="bank")
-        nc.tensor.transpose(bank[:, 0, :], result[:], ident[:])
-        out_rows = keep.tile([ROWS, P], F32)
-        nc.vector.tensor_copy(out=out_rows[:], in_=bank[0:ROWS, 0, :])
         nc.sync.dma_start(out=out.rearrange("b h (t p) -> (b h t) p", p=P), in_=out_rows[:])

@@ -41,8 +41,6 @@ def tile_multiheadenergyattention_pa_t_e_kernel(
         psum = stack.enter_context(tc.psum_pool(name="psum", bufs=BANKS))
         stack.enter_context(tc.manual_schedule())
 
-        beta_bf = keep.tile([P, 1], BF16)
-        nc.sync.dma_start(out=beta_bf[:], in_=betas.partition_broadcast(P))
         ident = keep.tile([P, P], F32)
         masks.make_identity(nc, ident[:])
         w_planes = keep.tile([P, 2, PASSES, HEAD], U8, align_bytes=64)
@@ -62,7 +60,6 @@ def tile_multiheadenergyattention_pa_t_e_kernel(
                 nc.sync.dma_start(out=x_sb[:, row, :], in_=x_rows[:, row, :])
 
         load_x(0)
-        load_x(1)
         w_codes = keep.tile([P, 2, PASSES, HEAD], U32, align_bytes=64)
         given = ((wq_words, wq_scales), (wk_words, wk_scales))
         for w in (K, Q):
@@ -76,13 +73,12 @@ def tile_multiheadenergyattention_pa_t_e_kernel(
                 out=w_codes[:, w, :, :].bitcast(I32),
                 in_=given[w][0].rearrange("g p n t -> p g (n t)").bitcast(I32),
             )
+        load_x(1)
+        beta_bf = keep.tile([P, 1], BF16)
+        nc.sync.dma_start(out=beta_bf[:], in_=betas.partition_broadcast(P))
         for b in range(2, BATCH):
             load_x(b)
 
-        neg_beta = keep.tile([P, 1], F32)
-        nc.vector.tensor_scalar_mul(out=neg_beta[:], in0=beta_bf[:], scalar1=-1.0)
-        neg_inv_beta = keep.tile([P, 1], F32)
-        nc.vector.reciprocal(out=neg_inv_beta[:], in_=neg_beta[:])
         off_diag = keep.tile([P, P], F32)
         nc.vector.tensor_scalar(
             out=off_diag[:], in0=ident[:], scalar1=BIG, scalar2=-BIG, op0=ALU.mult, op1=ALU.add
@@ -91,18 +87,25 @@ def tile_multiheadenergyattention_pa_t_e_kernel(
         nc.vector.scalar_tensor_tensor(
             out=diag_mask[:], in0=ident[:], scalar=MASKED, in1=off_diag[:], op0=ALU.mult, op1=ALU.add
         )
+        neg_beta = keep.tile([P, 1], F32)
+        neg_inv_beta = keep.tile([P, 1], F32)
+
+        def negate_beta():
+            nc.vector.tensor_scalar_mul(out=neg_beta[:], in0=beta_bf[:], scalar1=-1.0)
+            nc.vector.reciprocal(out=neg_inv_beta[:], in_=neg_beta[:])
 
         x_grouped, x_codes, x_scales = {}, {}, {}
         qk_grouped, qk_codes, qk_scales = {}, {}, {}
         score_bank, neg_scores, diag_min, rest_min = {}, {}, {}, {}
 
 
-        def transpose_x(b):
+        def transpose_x(b, tiles, scalar_tiles):
             if not 0 <= b < BATCH:
                 return
-            grouped = ring.tile([P, PASSES, TOKENS, PACK], BF16, align_bytes=64, name="x_grouped")
-            grouped_words = grouped[:].bitcast(F32)
-            for t in range(TILES):
+            if b not in x_grouped:
+                x_grouped[b] = ring.tile([P, TILES, PASSES, P, PACK], BF16, align_bytes=64, name="x_grouped")
+            grouped_words = x_grouped[b][:].bitcast(F32)
+            for t in tiles:
                 words = x_sb[:, b * TILES + t, :].bitcast(F32)
                 bank = psum.tile([P, 2 * PASSES, P], F32, name="bank")
                 for g in range(PASSES):
@@ -111,21 +114,21 @@ def tile_multiheadenergyattention_pa_t_e_kernel(
                             bank[:, 2 * g + u, :], words[:, WORDS * g + u : WORDS * (g + 1) : 2], ident[:]
                         )
                 planes = bank[:].rearrange("p (g u) r -> p g r u", u=2)
-                if t < TILES - 1:
-                    nc.vector.tensor_copy(out=grouped_words[:, :, t * P : (t + 1) * P, :], in_=planes)
+                if t in scalar_tiles:
+                    nc.scalar.copy(out=grouped_words[:, t, :, :, :], in_=planes)
                 else:
-                    nc.scalar.copy(out=grouped_words[:, :, t * P : (t + 1) * P, :], in_=planes)
-            x_grouped[b] = grouped
+                    nc.vector.tensor_copy(out=grouped_words[:, t, :, :, :], in_=planes)
 
-        def quantise_x(b):
+        def quantise_x(b, tiles):
             if not 0 <= b < BATCH:
                 return
-            x_codes[b] = ring.tile([P, PASSES, TOKENS], U32, align_bytes=64, name="x_codes")
-            x_scales[b] = ring.tile([P, PASSES, TOKENS], U8, align_bytes=64, name="x_scales")
+            if b not in x_codes:
+                x_codes[b] = ring.tile([P, TILES, PASSES, P], U32, align_bytes=64, name="x_codes")
+                x_scales[b] = ring.tile([P, TILES, PASSES, P], U8, align_bytes=64, name="x_scales")
             nc.vector.quantize_mx(
-                out=x_codes[b][:].rearrange("p g r -> p (g r)").bitcast(FP8X4),
-                scales=x_scales[b][:].rearrange("p g r -> p (g r)"),
-                in_=x_grouped[b][:].rearrange("p g r t -> p (g r t)"),
+                out=x_codes[b][:, tiles, :, :].rearrange("p t g r -> p (t g r)").bitcast(FP8X4),
+                scales=x_scales[b][:, tiles, :, :].rearrange("p t g r -> p (t g r)"),
+                in_=x_grouped[b][:, tiles, :, :, :].rearrange("p t g r k -> p (t g r k)"),
             )
 
         def project(b, w, t):
@@ -140,8 +143,8 @@ def tile_multiheadenergyattention_pa_t_e_kernel(
                         out=bank[:, z, :],
                         lhsT=w_codes[:, w, g, heads].bitcast(FP8X4),
                         lhsT_scale=w_planes[:, w, g, heads],
-                        rhs=x_codes[b][:, g, tokens].bitcast(FP8X4),
-                        rhs_scale=x_scales[b][:, g, tokens],
+                        rhs=x_codes[b][:, t, g, :].bitcast(FP8X4),
+                        rhs_scale=x_scales[b][:, t, g, :],
                         start=(g == 0),
                         stop=(g == PASSES - 1),
                     )
@@ -162,11 +165,12 @@ def tile_multiheadenergyattention_pa_t_e_kernel(
             b, n = divmod(row, TILES)
             queries = slice(n * P, (n + 1) * P)
             bank = psum.tile([P, TILES, P], F32, name="bank")
-            for j in range(TILES):
-                m = (n + j) % TILES
-                keys = slice(m * P, (m + 1) * P)
+            own = n // 2
+            for j in range(2):
+                pair = (own + j + n) % 2
+                keys = slice(2 * pair * P, 2 * (pair + 1) * P)
                 nc.tensor.matmul_mx(
-                    out=bank[:, j, :],
+                    out=bank[:, 2 * j : 2 * j + 2, :].rearrange("p j r -> p (j r)"),
                     lhsT=qk_codes[b][:, Q, queries].bitcast(FP8X4),
                     lhsT_scale=qk_scales[b][:, Q, queries],
                     rhs=qk_codes[b][:, K, keys].bitcast(FP8X4),
@@ -182,10 +186,12 @@ def tile_multiheadenergyattention_pa_t_e_kernel(
             neg = pairs.tile([P, 2, TOKENS], F32, name="neg")
             diag_min[first] = pairs.tile([P, 2], F32, name="diag_min")
             rest_min[first] = pairs.tile([P, 2], F32, name="rest_min")
+            own_tile = (0, TILES - 1)
+            other_tiles = (slice(1, TILES), slice(0, TILES - 1))
             for i in range(2):
                 nc.vector.scalar_tensor_tensor(
                     out=neg[:, i, 0:P],
-                    in0=score_bank[first + i][:, 0, :],
+                    in0=score_bank[first + i][:, own_tile[i], :],
                     scalar=neg_beta[:, 0:1],
                     in1=diag_mask[:],
                     op0=ALU.mult,
@@ -194,7 +200,7 @@ def tile_multiheadenergyattention_pa_t_e_kernel(
             for i in range(2):
                 nc.vector.tensor_scalar(
                     out=neg[:, i, P:TOKENS],
-                    in0=score_bank[first + i][:, 1:TILES, :].rearrange("p j r -> p (j r)"),
+                    in0=score_bank[first + i][:, other_tiles[i], :].rearrange("p j r -> p (j r)"),
                     scalar1=neg_beta[:, 0:1],
                     scalar2=None,
                     op0=ALU.mult,
@@ -225,33 +231,54 @@ def tile_multiheadenergyattention_pa_t_e_kernel(
                 accum_out=exp_sums[:, row : row + 1],
             )
 
-        def quarter(b, w, t, row):
-            project(b, w, t)
-            project(b, w, t + 1)
-            scores(row)
-            exp_sum(row - 4)
-
         first_half, second_half = slice(0, TOKENS // 2), slice(TOKENS // 2, TOKENS)
-        for step in range(BATCH + 4):
-            b = step - 2
-            row = (step - 3) * TILES
-            if 0 <= b < BATCH:
-                qk_grouped[b] = ring.tile([P, 2, TOKENS, PACK], BF16, align_bytes=64, name="qk_grouped")
-                qk_codes[b] = ring.tile([P, 2, TOKENS], U32, align_bytes=64, name="qk_codes")
-                qk_scales[b] = ring.tile([P, 2, TOKENS], U8, align_bytes=64, name="qk_scales")
-            quantise_x(step - 1)
+        first_tiles, second_tiles = slice(0, TILES // 2), slice(TILES // 2, TILES)
+
+        def open_qk(b):
+            if not 0 <= b < BATCH:
+                return
+            qk_grouped[b] = ring.tile([P, 2, TOKENS, PACK], BF16, align_bytes=64, name="qk_grouped")
+            qk_codes[b] = ring.tile([P, 2, TOKENS], U32, align_bytes=64, name="qk_codes")
+            qk_scales[b] = ring.tile([P, 2, TOKENS], U8, align_bytes=64, name="qk_scales")
+
+        transpose_x(0, (0, 1), (1,))
+        transpose_x(0, (2, 3), (3,))
+        quantise_x(0, first_tiles)
+        quantise_x(0, second_tiles)
+        for b in range(BATCH + 1):
+            row = (b - 1) * TILES
+            if b == 1:
+                negate_beta()
+            open_qk(b)
+            project(b, K, 0)
+            project(b, K, 1)
+            scores(row)
             join_min(row - 2)
-            quarter(b, K, 0, row)
-            quarter(b, K, 2, row + 1)
+            exp_sum(row - 2)
+            project(b, K, 2)
+            project(b, K, 3)
+            exp_sum(row - 1)
+            scores(row + 1)
             mask_and_min(row)
             quantise_qk(b, K, slice(0, TOKENS))
+            transpose_x(b + 1, (0, 1, 2, 3), (3,))
             join_min(row)
-            quarter(b, Q, 0, row + 2)
+            project(b, Q, 0)
+            project(b, Q, 1)
+            exp_sum(row)
+            scores(row + 2)
+            quantise_x(b + 1, first_tiles)
             quantise_qk(b, Q, first_half)
-            quarter(b, Q, 2, row + 3)
+            project(b, Q, 2)
+            project(b, Q, 3)
+            exp_sum(row + 1)
+            scores(row + 3)
+            quantise_x(b + 1, second_tiles)
             mask_and_min(row + 2)
             quantise_qk(b, Q, second_half)
-            transpose_x(step)
+        join_min(BATCH * TILES - 2)
+        exp_sum(BATCH * TILES - 2)
+        exp_sum(BATCH * TILES - 1)
 
         nc.scalar.activation(out=warm[:], in_=warm[:], func=ACT.Ln)
         top_bank = psum.tile([P, PACK, P], F32, name="bank")

@@ -23,6 +23,9 @@ PASSES = FEATURES // (P * PACK)
 WORDS = P * PACK // 2
 ROWS = BATCH * TILES
 BANKS = 8
+LINE = TOKENS + 8
+OWN_TILE = (0, TILES - 1)
+OTHER_TILES = (slice(1, TILES), slice(0, TILES - 1))
 Q, K = 0, 1
 MASKED = 1.0e9
 BIG = 3.0e38
@@ -59,21 +62,24 @@ def tile_multiheadenergyattention_pa_t_e_kernel(
             for row in range(b * TILES, (b + 1) * TILES):
                 nc.sync.dma_start(out=x_sb[:, row, :], in_=x_rows[:, row, :])
 
-        load_x(0)
         w_codes = keep.tile([P, 2, PASSES, HEAD], U32, align_bytes=64)
         given = ((wq_words, wq_scales), (wk_words, wk_scales))
-        for w in (K, Q):
+
+        def load_weights(w):
             for i in range(4):
                 nc.sync.dma_start(
                     out=w_planes[32 * i : 32 * i + 4, w, :, :].bitcast(I32),
                     in_=given[w][1][:, 4 * i : 4 * i + 4, :].rearrange("g r n -> r g n").bitcast(I32),
                 )
-        for w in (K, Q):
             nc.sync.dma_start(
                 out=w_codes[:, w, :, :].bitcast(I32),
                 in_=given[w][0].rearrange("g p n t -> p g (n t)").bitcast(I32),
             )
+
+        load_x(0)
+        load_weights(K)
         load_x(1)
+        load_weights(Q)
         beta_bf = keep.tile([P, 1], BF16)
         nc.sync.dma_start(out=beta_bf[:], in_=betas.partition_broadcast(P))
         for b in range(2, BATCH):
@@ -96,7 +102,7 @@ def tile_multiheadenergyattention_pa_t_e_kernel(
 
         x_grouped, x_codes, x_scales = {}, {}, {}
         qk_grouped, qk_codes, qk_scales = {}, {}, {}
-        score_bank, neg_scores, diag_min, rest_min = {}, {}, {}, {}
+        score_bank, lines = {}, {}
 
 
         def transpose_x(b, tiles, scalar_tiles):
@@ -180,18 +186,14 @@ def tile_multiheadenergyattention_pa_t_e_kernel(
                 )
             score_bank[row] = bank
 
-        def mask_and_min(first):
+        def negate_and_mask(first):
             if not 0 <= first < ROWS:
                 return
-            neg = pairs.tile([P, 2, TOKENS], F32, name="neg")
-            diag_min[first] = pairs.tile([P, 2], F32, name="diag_min")
-            rest_min[first] = pairs.tile([P, 2], F32, name="rest_min")
-            own_tile = (0, TILES - 1)
-            other_tiles = (slice(1, TILES), slice(0, TILES - 1))
+            lines[first] = pairs.tile([P, 2, LINE], F32, name="neg")
             for i in range(2):
                 nc.vector.scalar_tensor_tensor(
-                    out=neg[:, i, 0:P],
-                    in0=score_bank[first + i][:, own_tile[i], :],
+                    out=lines[first][:, i, 1 : 1 + P],
+                    in0=score_bank[first + i][:, OWN_TILE[i], :],
                     scalar=neg_beta[:, 0:1],
                     in1=diag_mask[:],
                     op0=ALU.mult,
@@ -199,32 +201,31 @@ def tile_multiheadenergyattention_pa_t_e_kernel(
                 )
             for i in range(2):
                 nc.vector.tensor_scalar(
-                    out=neg[:, i, P:TOKENS],
-                    in0=score_bank[first + i][:, other_tiles[i], :].rearrange("p j r -> p (j r)"),
+                    out=lines[first][:, i, 1 + P : 1 + TOKENS],
+                    in0=score_bank[first + i][:, OTHER_TILES[i], :].rearrange("p j r -> p (j r)"),
                     scalar1=neg_beta[:, 0:1],
                     scalar2=None,
                     op0=ALU.mult,
                     op1=ALU.min,
-                    accum_out=rest_min[first][:, i : i + 1],
+                    accum_out=lines[first][:, i, 0:1],
                 )
-                neg_scores[first + i] = neg[:, i, :]
-            nc.vector.tensor_reduce(
-                out=diag_min[first][:], in_=neg[:, :, 0:P], axis=mybir.AxisListType.X, op=ALU.min
-            )
 
-        def join_min(first):
+        def find_top(first):
             if not 0 <= first < ROWS:
                 return
-            nc.vector.tensor_tensor(
-                out=neg_top[:, first : first + 2], in0=diag_min[first][:], in1=rest_min[first][:], op=ALU.min
+            nc.vector.tensor_reduce(
+                out=neg_top[:, first : first + 2],
+                in_=lines[first][:, :, 0 : 1 + P],
+                axis=mybir.AxisListType.X,
+                op=ALU.min,
             )
 
         def exp_sum(row):
             if not 0 <= row < ROWS:
                 return
             nc.scalar.activation(
-                out=neg_scores[row],
-                in_=neg_scores[row],
+                out=lines[row - row % 2][:, row % 2, 1 : 1 + TOKENS],
+                in_=lines[row - row % 2][:, row % 2, 1 : 1 + TOKENS],
                 func=ACT.Exp,
                 bias=neg_top[:, row : row + 1],
                 scale=-1.0,
@@ -253,30 +254,30 @@ def tile_multiheadenergyattention_pa_t_e_kernel(
             project(b, K, 0)
             project(b, K, 1)
             scores(row)
-            join_min(row - 2)
-            exp_sum(row - 2)
+            exp_sum(row - 3)
             project(b, K, 2)
             project(b, K, 3)
-            exp_sum(row - 1)
+            exp_sum(row - 2)
             scores(row + 1)
-            mask_and_min(row)
+            negate_and_mask(row)
             quantise_qk(b, K, slice(0, TOKENS))
+            find_top(row)
             transpose_x(b + 1, (0, 1, 2, 3), (3,))
-            join_min(row)
             project(b, Q, 0)
             project(b, Q, 1)
-            exp_sum(row)
+            exp_sum(row - 1)
             scores(row + 2)
             quantise_x(b + 1, first_tiles)
             quantise_qk(b, Q, first_half)
             project(b, Q, 2)
             project(b, Q, 3)
-            exp_sum(row + 1)
+            exp_sum(row)
             scores(row + 3)
             quantise_x(b + 1, second_tiles)
-            mask_and_min(row + 2)
+            negate_and_mask(row + 2)
             quantise_qk(b, Q, second_half)
-        join_min(BATCH * TILES - 2)
+            find_top(row + 2)
+        exp_sum(BATCH * TILES - 3)
         exp_sum(BATCH * TILES - 2)
         exp_sum(BATCH * TILES - 1)
 

@@ -55,6 +55,20 @@ def tile_multiheadenergyattention_pa_t_e_kernel(
         warm = keep.tile([P, 1], F32)
         nc.scalar.activation(out=warm[:], in_=neg_top[:, 0:1], func=ACT.Exp)
 
+        idle = keep.tile([P, TOKENS], BF16)
+        nc.gpsimd.memset(idle[:], 0.0)
+
+        def keep_warm(count):
+            bank = psum.tile([P, TILES, P], F32, name="bank")
+            for i in range(count):
+                nc.tensor.matmul(
+                    out=bank[:].rearrange("p j r -> p (j r)"),
+                    lhsT=idle[:, 0:P],
+                    rhs=idle[:],
+                    start=True,
+                    stop=True,
+                )
+
         x_sb = keep.tile([P, ROWS, FEATURES], BF16)
         x_rows = x.rearrange("b (t p) d -> p (b t) d", p=P)
 
@@ -105,6 +119,17 @@ def tile_multiheadenergyattention_pa_t_e_kernel(
         score_bank, lines = {}, {}
 
 
+        x_sorted = {}
+
+        def sort_words(b, t):
+            if not 0 <= b < BATCH:
+                return
+            x_sorted[b, t] = ring.tile([P, FEATURES], BF16, align_bytes=64, name="x_sorted_%d" % t)
+            nc.vector.tensor_copy(
+                out=x_sorted[b, t][:].bitcast(F32).rearrange("p (g u m) -> p g u m", g=PASSES, u=2),
+                in_=x_sb[:, b * TILES + t, :].bitcast(F32).rearrange("p (g m u) -> p g u m", g=PASSES, u=2),
+            )
+
         def transpose_x(b, tiles, scalar_tiles):
             if not 0 <= b < BATCH:
                 return
@@ -112,13 +137,18 @@ def tile_multiheadenergyattention_pa_t_e_kernel(
                 x_grouped[b] = ring.tile([P, TILES, PASSES, P, PACK], BF16, align_bytes=64, name="x_grouped")
             grouped_words = x_grouped[b][:].bitcast(F32)
             for t in tiles:
-                words = x_sb[:, b * TILES + t, :].bitcast(F32)
+                if (b, t) in x_sorted:
+                    words = x_sorted[b, t][:].bitcast(F32)
+                else:
+                    words = x_sb[:, b * TILES + t, :].bitcast(F32)
                 bank = psum.tile([P, 2 * PASSES, P], F32, name="bank")
                 for g in range(PASSES):
                     for u in range(2):
-                        nc.tensor.transpose(
-                            bank[:, 2 * g + u, :], words[:, WORDS * g + u : WORDS * (g + 1) : 2], ident[:]
-                        )
+                        if (b, t) in x_sorted:
+                            plane = words[:, (2 * g + u) * P : (2 * g + u + 1) * P]
+                        else:
+                            plane = words[:, WORDS * g + u : WORDS * (g + 1) : 2]
+                        nc.tensor.transpose(bank[:, 2 * g + u, :], plane, ident[:])
                 planes = bank[:].rearrange("p (g u) r -> p g r u", u=2)
                 if t in scalar_tiles:
                     nc.scalar.copy(out=grouped_words[:, t, :, :, :], in_=planes)
@@ -154,7 +184,10 @@ def tile_multiheadenergyattention_pa_t_e_kernel(
                         start=(g == 0),
                         stop=(g == PASSES - 1),
                     )
-            nc.scalar.copy(out=qk_grouped[b][:, w, tokens, :], in_=bank[:].rearrange("p z r -> p r z"))
+            if b == BATCH - 1 and (w, t) == (K, TILES - 1):
+                nc.vector.tensor_copy(out=qk_grouped[b][:, w, tokens, :], in_=bank[:].rearrange("p z r -> p r z"))
+            else:
+                nc.scalar.copy(out=qk_grouped[b][:, w, tokens, :], in_=bank[:].rearrange("p z r -> p r z"))
 
         def quantise_qk(b, w, tokens):
             if not 0 <= b < BATCH:
@@ -186,11 +219,12 @@ def tile_multiheadenergyattention_pa_t_e_kernel(
                 )
             score_bank[row] = bank
 
-        def negate_and_mask(first):
+        def negate_and_mask(first, pair=(0, 1)):
             if not 0 <= first < ROWS:
                 return
-            lines[first] = pairs.tile([P, 2, LINE], F32, name="neg")
-            for i in range(2):
+            if first not in lines:
+                lines[first] = pairs.tile([P, 2, LINE], F32, name="neg")
+            for i in pair:
                 nc.vector.scalar_tensor_tensor(
                     out=lines[first][:, i, 1 : 1 + P],
                     in0=score_bank[first + i][:, OWN_TILE[i], :],
@@ -199,7 +233,7 @@ def tile_multiheadenergyattention_pa_t_e_kernel(
                     op0=ALU.mult,
                     op1=ALU.max,
                 )
-            for i in range(2):
+            for i in pair:
                 nc.vector.tensor_scalar(
                     out=lines[first][:, i, 1 + P : 1 + TOKENS],
                     in0=score_bank[first + i][:, OTHER_TILES[i], :].rearrange("p j r -> p (j r)"),
@@ -210,12 +244,12 @@ def tile_multiheadenergyattention_pa_t_e_kernel(
                     accum_out=lines[first][:, i, 0:1],
                 )
 
-        def find_top(first):
+        def find_top(first, pair=(0, 1)):
             if not 0 <= first < ROWS:
                 return
             nc.vector.tensor_reduce(
-                out=neg_top[:, first : first + 2],
-                in_=lines[first][:, :, 0 : 1 + P],
+                out=neg_top[:, first + pair[0] : first + pair[-1] + 1],
+                in_=lines[first][:, pair[0] : pair[-1] + 1, 0 : 1 + P],
                 axis=mybir.AxisListType.X,
                 op=ALU.min,
             )
@@ -242,8 +276,10 @@ def tile_multiheadenergyattention_pa_t_e_kernel(
             qk_codes[b] = ring.tile([P, 2, TOKENS], U32, align_bytes=64, name="qk_codes")
             qk_scales[b] = ring.tile([P, 2, TOKENS], U8, align_bytes=64, name="qk_scales")
 
+        keep_warm(3)
         transpose_x(0, (0, 1), (1,))
         transpose_x(0, (2, 3), (3,))
+        keep_warm(4)
         quantise_x(0, first_tiles)
         quantise_x(0, second_tiles)
         for b in range(BATCH + 1):
@@ -268,15 +304,22 @@ def tile_multiheadenergyattention_pa_t_e_kernel(
             exp_sum(row - 1)
             scores(row + 2)
             quantise_x(b + 1, first_tiles)
+            quantise_x(b + 1, second_tiles)
             quantise_qk(b, Q, first_half)
             project(b, Q, 2)
             project(b, Q, 3)
             exp_sum(row)
             scores(row + 3)
-            quantise_x(b + 1, second_tiles)
-            negate_and_mask(row + 2)
-            quantise_qk(b, Q, second_half)
-            find_top(row + 2)
+            if b < BATCH:
+                negate_and_mask(row + 2)
+                quantise_qk(b, Q, second_half)
+                find_top(row + 2)
+            else:
+                for i in range(2):
+                    negate_and_mask(row + 2, (i,))
+                    find_top(row + 2, (i,))
+            for t in range(TILES if b == 0 else 0):
+                sort_words(b + 2, t)
         exp_sum(BATCH * TILES - 3)
         exp_sum(BATCH * TILES - 2)
         exp_sum(BATCH * TILES - 1)

@@ -85,10 +85,9 @@ def tile_multiheadenergyattention_pa_t_e_kernel(
                     out=w_planes[32 * i : 32 * i + 4, w, :, :].bitcast(I32),
                     in_=given[w][1][:, 4 * i : 4 * i + 4, :].rearrange("g r n -> r g n").bitcast(I32),
                 )
-            nc.sync.dma_start(
-                out=w_codes[:, w, :, :].bitcast(I32),
-                in_=given[w][0].rearrange("g p n t -> p g (n t)").bitcast(I32),
-            )
+            words = given[w][0].rearrange("g p n t -> p g (n t)").bitcast(I32)
+            for half in (slice(0, HEAD // 2), slice(HEAD // 2, HEAD)):
+                nc.sync.dma_start(out=w_codes[:, w, :, half].bitcast(I32), in_=words[:, :, half])
 
         load_x(0)
         load_weights(K)
@@ -282,6 +281,8 @@ def tile_multiheadenergyattention_pa_t_e_kernel(
         keep_warm(4)
         quantise_x(0, first_tiles)
         quantise_x(0, second_tiles)
+        for t in range(TILES):
+            sort_words(1, t)
         for b in range(BATCH + 1):
             row = (b - 1) * TILES
             if b == 1:
@@ -318,7 +319,7 @@ def tile_multiheadenergyattention_pa_t_e_kernel(
                 for i in range(2):
                     negate_and_mask(row + 2, (i,))
                     find_top(row + 2, (i,))
-            for t in range(TILES if b == 0 else 0):
+            for t in range(2 if b == 0 else 0):
                 sort_words(b + 2, t)
         exp_sum(BATCH * TILES - 3)
         exp_sum(BATCH * TILES - 2)

@@ -44,17 +44,6 @@ def tile_multiheadenergyattention_pa_t_e_kernel(
         psum = stack.enter_context(tc.psum_pool(name="psum", bufs=BANKS))
         stack.enter_context(tc.manual_schedule())
 
-        ident = keep.tile([P, P], F32)
-        masks.make_identity(nc, ident[:])
-        w_planes = keep.tile([P, 2, PASSES, HEAD], U8, align_bytes=64)
-        nc.vector.memset(w_planes[:].rearrange("p w g n -> p (w g n)").bitcast(I32), 0)
-        neg_top = keep.tile([P, P], F32)
-        exp_sums = keep.tile([P, P], F32)
-        nc.vector.memset(neg_top[:], 0.0)
-        nc.vector.memset(exp_sums[:], 0.0)
-        warm = keep.tile([P, 1], F32)
-        nc.scalar.activation(out=warm[:], in_=neg_top[:, 0:1], func=ACT.Exp)
-
         idle = keep.tile([P, TOKENS], BF16)
         nc.gpsimd.memset(idle[:], 0.0)
 
@@ -68,6 +57,17 @@ def tile_multiheadenergyattention_pa_t_e_kernel(
                     start=True,
                     stop=True,
                 )
+
+        ident = keep.tile([P, P], F32)
+        masks.make_identity(nc, ident[:])
+        w_planes = keep.tile([P, 2, PASSES, HEAD], U8, align_bytes=64)
+        nc.vector.memset(w_planes[:].rearrange("p w g n -> p (w g n)").bitcast(I32), 0)
+        neg_top = keep.tile([P, P], F32)
+        exp_sums = keep.tile([P, P], F32)
+        nc.vector.memset(neg_top[:], 0.0)
+        nc.vector.memset(exp_sums[:], 0.0)
+        warm = keep.tile([P, 1], F32)
+        nc.scalar.activation(out=warm[:], in_=neg_top[:, 0:1], func=ACT.Exp)
 
         x_sb = keep.tile([P, ROWS, FEATURES], BF16)
         x_rows = x.rearrange("b (t p) d -> p (b t) d", p=P)
@@ -275,7 +275,7 @@ def tile_multiheadenergyattention_pa_t_e_kernel(
             qk_codes[b] = ring.tile([P, 2, TOKENS], U32, align_bytes=64, name="qk_codes")
             qk_scales[b] = ring.tile([P, 2, TOKENS], U8, align_bytes=64, name="qk_scales")
 
-        keep_warm(3)
+        keep_warm(4)
         transpose_x(0, (0, 1), (1,))
         transpose_x(0, (2, 3), (3,))
         keep_warm(4)
@@ -296,8 +296,9 @@ def tile_multiheadenergyattention_pa_t_e_kernel(
             project(b, K, 3)
             exp_sum(row - 2)
             scores(row + 1)
+            quantise_qk(b, K, first_half)
             negate_and_mask(row)
-            quantise_qk(b, K, slice(0, TOKENS))
+            quantise_qk(b, K, second_half)
             find_top(row)
             transpose_x(b + 1, (0, 1, 2, 3), (3,))
             project(b, Q, 0)

@@ -120,11 +120,11 @@ def tile_multiheadenergyattention_pa_t_e_kernel(
 
         x_sorted = {}
 
-        def sort_words(b, t):
+        def sort_words(b, t, on_scalar=False):
             if not 0 <= b < BATCH:
                 return
             x_sorted[b, t] = ring.tile([P, FEATURES], BF16, align_bytes=64, name="x_sorted_%d" % t)
-            nc.vector.tensor_copy(
+            (nc.scalar.copy if on_scalar else nc.vector.tensor_copy)(
                 out=x_sorted[b, t][:].bitcast(F32).rearrange("p (g u m) -> p g u m", g=PASSES, u=2),
                 in_=x_sb[:, b * TILES + t, :].bitcast(F32).rearrange("p (g m u) -> p g u m", g=PASSES, u=2),
             )
@@ -295,6 +295,8 @@ def tile_multiheadenergyattention_pa_t_e_kernel(
             project(b, K, 2)
             project(b, K, 3)
             exp_sum(row - 2)
+            if b >= 1:
+                sort_words(b + 2, 0, on_scalar=True)
             scores(row + 1)
             quantise_qk(b, K, first_half)
             negate_and_mask(row)

from contextlib import ExitStack

import concourse.masks as masks
import concourse.mybir as mybir

F32 = mybir.dt.float32
BF16 = mybir.dt.bfloat16
I32 = mybir.dt.int32
U32 = mybir.dt.uint32
U8 = mybir.dt.uint8
FP8X4 = mybir.dt.float8_e4m3fn_x4
ALU = mybir.AluOpType
ACT = mybir.ActivationFunctionType

P = 128
PACK = 4
BATCH = 8
TOKENS = 512
FEATURES = 1024
HEAD = 512
TILES = TOKENS // P
PASSES = FEATURES // (P * PACK)
WORDS = P * PACK // 2
ROWS = BATCH * TILES
BANKS = 8
LINE = TOKENS + 8
OWN_TILE = (0, TILES - 1)
OTHER_TILES = (slice(1, TILES), slice(0, TILES - 1))
Q, K = 0, 1
MASKED = 1.0e9
BIG = 3.0e38

FLOPS = 2 * BATCH * TOKENS * FEATURES * HEAD * 2 + 2 * BATCH * TOKENS * TOKENS * HEAD


def tile_multiheadenergyattention_pa_t_e_kernel(
    tc, x, wk_words, wk_scales, wq_words, wq_scales, betas, out
):
    nc = tc.nc
    with ExitStack() as stack:
        keep = stack.enter_context(tc.tile_pool(name="keep", bufs=1))
        ring = stack.enter_context(tc.tile_pool(name="ring", bufs=2))
        pairs = stack.enter_context(tc.tile_pool(name="pairs", bufs=4))
        psum = stack.enter_context(tc.psum_pool(name="psum", bufs=BANKS))
        stack.enter_context(tc.manual_schedule())

        idle = keep.tile([P, TOKENS], BF16)
        nc.gpsimd.memset(idle[:], 0.0)

        def keep_warm(count):
            bank = psum.tile([P, TILES, P], F32, name="bank")
            for i in range(count):
                nc.tensor.matmul(
                    out=bank[:].rearrange("p j r -> p (j r)"),
                    lhsT=idle[:, 0:P],
                    rhs=idle[:],
                    start=True,
                    stop=True,
                )

        ident = keep.tile([P, P], F32)
        masks.make_identity(nc, ident[:])
        w_planes = keep.tile([P, 2, PASSES, HEAD], U8, align_bytes=64)
        nc.vector.memset(w_planes[:].rearrange("p w g n -> p (w g n)").bitcast(I32), 0)
        neg_top = keep.tile([P, P], F32)
        exp_sums = keep.tile([P, P], F32)
        nc.vector.memset(neg_top[:], 0.0)
        nc.vector.memset(exp_sums[:], 0.0)
        warm = keep.tile([P, 1], F32)
        nc.scalar.activation(out=warm[:], in_=neg_top[:, 0:1], func=ACT.Exp)

        x_sb = keep.tile([P, ROWS, FEATURES], BF16)
        x_rows = x.rearrange("b (t p) d -> p (b t) d", p=P)

        def load_x(b):
            for row in range(b * TILES, (b + 1) * TILES):
                nc.sync.dma_start(out=x_sb[:, row, :], in_=x_rows[:, row, :])

        w_codes = keep.tile([P, 2, PASSES, HEAD], U32, align_bytes=64)
        given = ((wq_words, wq_scales), (wk_words, wk_scales))

        def load_weights(w):
            for i in range(4):
                nc.sync.dma_start(
                    out=w_planes[32 * i : 32 * i + 4, w, :, :].bitcast(I32),
                    in_=given[w][1][:, 4 * i : 4 * i + 4, :].rearrange("g r n -> r g n").bitcast(I32),
                )
            words = given[w][0].rearrange("g p n t -> p g (n t)").bitcast(I32)
            for half in (slice(0, HEAD // 2), slice(HEAD // 2, HEAD)):
                nc.sync.dma_start(out=w_codes[:, w, :, half].bitcast(I32), in_=words[:, :, half])

        load_x(0)
        load_weights(K)
        load_x(1)
        load_weights(Q)
        beta_bf = keep.tile([P, 1], BF16)
        nc.sync.dma_start(out=beta_bf[:], in_=betas.partition_broadcast(P))
        for b in range(2, BATCH):
            load_x(b)

        off_diag = keep.tile([P, P], F32)
        nc.vector.tensor_scalar(
            out=off_diag[:], in0=ident[:], scalar1=BIG, scalar2=-BIG, op0=ALU.mult, op1=ALU.add
        )
        diag_mask = keep.tile([P, P], F32)
        nc.vector.scalar_tensor_tensor(
            out=diag_mask[:], in0=ident[:], scalar=MASKED, in1=off_diag[:], op0=ALU.mult, op1=ALU.add
        )
        neg_beta = keep.tile([P, 1], F32)
        neg_inv_beta = keep.tile([P, 1], F32)

        def negate_beta():
            nc.vector.tensor_scalar_mul(out=neg_beta[:], in0=beta_bf[:], scalar1=-1.0)
            nc.vector.reciprocal(out=neg_inv_beta[:], in_=neg_beta[:])

        x_grouped, x_codes, x_scales = {}, {}, {}
        qk_grouped, qk_codes, qk_scales = {}, {}, {}
        score_bank, lines = {}, {}


        x_sorted = {}

        def sort_words(b, t, on_scalar=False):
            if not 0 <= b < BATCH:
                return
            x_sorted[b, t] = ring.tile([P, FEATURES], BF16, align_bytes=64, name="x_sorted_%d" % t)
            (nc.scalar.copy if on_scalar else nc.vector.tensor_copy)(
                out=x_sorted[b, t][:].bitcast(F32).rearrange("p (g u m) -> p g u m", g=PASSES, u=2),
                in_=x_sb[:, b * TILES + t, :].bitcast(F32).rearrange("p (g m u) -> p g u m", g=PASSES, u=2),
            )

        def transpose_x(b, tiles, scalar_tiles):
            if not 0 <= b < BATCH:
                return
            if b not in x_grouped:
                x_grouped[b] = ring.tile([P, TILES, PASSES, P, PACK], BF16, align_bytes=64, name="x_grouped")
            grouped_words = x_grouped[b][:].bitcast(F32)
            for t in tiles:
                if (b, t) in x_sorted:
                    words = x_sorted[b, t][:].bitcast(F32)
                else:
                    words = x_sb[:, b * TILES + t, :].bitcast(F32)
                bank = psum.tile([P, 2 * PASSES, P], F32, name="bank")
                for g in range(PASSES):
                    for u in range(2):
                        if (b, t) in x_sorted:
                            plane = words[:, (2 * g + u) * P : (2 * g + u + 1) * P]
                        else:
                            plane = words[:, WORDS * g + u : WORDS * (g + 1) : 2]
                        nc.tensor.transpose(bank[:, 2 * g + u, :], plane, ident[:])
                planes = bank[:].rearrange("p (g u) r -> p g r u", u=2)
                if t in scalar_tiles:
                    nc.scalar.copy(out=grouped_words[:, t, :, :, :], in_=planes)
                else:
                    nc.vector.tensor_copy(out=grouped_words[:, t, :, :, :], in_=planes)

        def quantise_x(b, tiles):
            if not 0 <= b < BATCH:
                return
            if b not in x_codes:
                x_codes[b] = ring.tile([P, TILES, PASSES, P], U32, align_bytes=64, name="x_codes")
                x_scales[b] = ring.tile([P, TILES, PASSES, P], U8, align_bytes=64, name="x_scales")
            nc.vector.quantize_mx(
                out=x_codes[b][:, tiles, :, :].rearrange("p t g r -> p (t g r)").bitcast(FP8X4),
                scales=x_scales[b][:, tiles, :, :].rearrange("p t g r -> p (t g r)"),
                in_=x_grouped[b][:, tiles, :, :, :].rearrange("p t g r k -> p (t g r k)"),
            )

        def project(b, w, t):
            if not 0 <= b < BATCH:
                return
            tokens = slice(t * P, (t + 1) * P)
            bank = psum.tile([P, PACK, P], F32, name="bank")
            for z in range(PACK):
                heads = slice(z * P, (z + 1) * P)
                for g in range(PASSES):
                    nc.tensor.matmul_mx(
                        out=bank[:, z, :],
                        lhsT=w_codes[:, w, g, heads].bitcast(FP8X4),
                        lhsT_scale=w_planes[:, w, g, heads],
                        rhs=x_codes[b][:, t, g, :].bitcast(FP8X4),
                        rhs_scale=x_scales[b][:, t, g, :],
                        start=(g == 0),
                        stop=(g == PASSES - 1),
                    )
            if b == BATCH - 1 and (w, t) == (K, TILES - 1):
                nc.vector.tensor_copy(out=qk_grouped[b][:, w, tokens, :], in_=bank[:].rearrange("p z r -> p r z"))
            else:
                nc.scalar.copy(out=qk_grouped[b][:, w, tokens, :], in_=bank[:].rearrange("p z r -> p r z"))

        def quantise_qk(b, w, tokens):
            if not 0 <= b < BATCH:
                return
            nc.vector.quantize_mx(
                out=qk_codes[b][:, w, tokens].bitcast(FP8X4),
                scales=qk_scales[b][:, w, tokens],
                in_=qk_grouped[b][:, w, tokens, :].rearrange("p r t -> p (r t)"),
            )

        def scores(row):
            if not 0 <= row < ROWS:
                return
            b, n = divmod(row, TILES)
            queries = slice(n * P, (n + 1) * P)
            bank = psum.tile([P, TILES, P], F32, name="bank")
            own = n // 2
            for j in range(2):
                pair = (own + j + n) % 2
                keys = slice(2 * pair * P, 2 * (pair + 1) * P)
                nc.tensor.matmul_mx(
                    out=bank[:, 2 * j : 2 * j + 2, :].rearrange("p j r -> p (j r)"),
                    lhsT=qk_codes[b][:, Q, queries].bitcast(FP8X4),
                    lhsT_scale=qk_scales[b][:, Q, queries],
                    rhs=qk_codes[b][:, K, keys].bitcast(FP8X4),
                    rhs_scale=qk_scales[b][:, K, keys],
                    start=True,
                    stop=True,
                )
            score_bank[row] = bank

        def negate_and_mask(first, pair=(0, 1)):
            if not 0 <= first < ROWS:
                return
            if first not in lines:
                lines[first] = pairs.tile([P, 2, LINE], F32, name="neg")
            for i in pair:
                nc.vector.scalar_tensor_tensor(
                    out=lines[first][:, i, 1 : 1 + P],
                    in0=score_bank[first + i][:, OWN_TILE[i], :],
                    scalar=neg_beta[:, 0:1],
                    in1=diag_mask[:],
                    op0=ALU.mult,
                    op1=ALU.max,
                )
            for i in pair:
                nc.vector.tensor_scalar(
                    out=lines[first][:, i, 1 + P : 1 + TOKENS],
                    in0=score_bank[first + i][:, OTHER_TILES[i], :].rearrange("p j r -> p (j r)"),
                    scalar1=neg_beta[:, 0:1],
                    scalar2=None,
                    op0=ALU.mult,
                    op1=ALU.min,
                    accum_out=lines[first][:, i, 0:1],
                )

        def find_top(first, pair=(0, 1)):
            if not 0 <= first < ROWS:
                return
            nc.vector.tensor_reduce(
                out=neg_top[:, first + pair[0] : first + pair[-1] + 1],
                in_=lines[first][:, pair[0] : pair[-1] + 1, 0 : 1 + P],
                axis=mybir.AxisListType.X,
                op=ALU.min,
            )

        def exp_sum(row):
            if not 0 <= row < ROWS:
                return
            nc.scalar.activation(
                out=lines[row - row % 2][:, row % 2, 1 : 1 + TOKENS],
                in_=lines[row - row % 2][:, row % 2, 1 : 1 + TOKENS],
                func=ACT.Exp,
                bias=neg_top[:, row : row + 1],
                scale=-1.0,
                accum_out=exp_sums[:, row : row + 1],
            )

        first_half, second_half = slice(0, TOKENS // 2), slice(TOKENS // 2, TOKENS)
        first_tiles, second_tiles = slice(0, TILES // 2), slice(TILES // 2, TILES)

        def open_qk(b):
            if not 0 <= b < BATCH:
                return
            qk_grouped[b] = ring.tile([P, 2, TOKENS, PACK], BF16, align_bytes=64, name="qk_grouped")
            qk_codes[b] = ring.tile([P, 2, TOKENS], U32, align_bytes=64, name="qk_codes")
            qk_scales[b] = ring.tile([P, 2, TOKENS], U8, align_bytes=64, name="qk_scales")

        keep_warm(4)
        transpose_x(0, (0, 1), (1,))
        transpose_x(0, (2, 3), (3,))
        keep_warm(4)
        quantise_x(0, first_tiles)
        quantise_x(0, second_tiles)
        for t in range(TILES):
            sort_words(1, t)
        for b in range(BATCH + 1):
            row = (b - 1) * TILES
            if b == 1:
                negate_beta()
            open_qk(b)
            project(b, K, 0)
            project(b, K, 1)
            scores(row)
            exp_sum(row - 3)
            project(b, K, 2)
            project(b, K, 3)
            exp_sum(row - 2)
            if b >= 1:
                sort_words(b + 2, 0, on_scalar=True)
            scores(row + 1)
            quantise_qk(b, K, first_half)
            negate_and_mask(row)
            quantise_qk(b, K, second_half)
            find_top(row)
            transpose_x(b + 1, (0, 1, 2, 3), (3,))
            project(b, Q, 0)
            project(b, Q, 1)
            exp_sum(row - 1)
            scores(row + 2)
            quantise_x(b + 1, first_tiles)
            quantise_x(b + 1, second_tiles)
            quantise_qk(b, Q, first_half)
            project(b, Q, 2)
            project(b, Q, 3)
            exp_sum(row)
            scores(row + 3)
            if b < BATCH:
                negate_and_mask(row + 2)
                quantise_qk(b, Q, second_half)
                find_top(row + 2)
            else:
                for i in range(2):
                    negate_and_mask(row + 2, (i,))
                    find_top(row + 2, (i,))
            for t in range(2 if b == 0 else 0):
                sort_words(b + 2, t)
        exp_sum(BATCH * TILES - 3)
        exp_sum(BATCH * TILES - 2)
        exp_sum(BATCH * TILES - 1)

        nc.scalar.activation(out=warm[:], in_=warm[:], func=ACT.Ln)
        top_bank = psum.tile([P, PACK, P], F32, name="bank")
        nc.tensor.transpose(top_bank[:, 0, :], neg_top[:], ident[:])
        top_over_beta = keep.tile([ROWS, P], F32)
        nc.vector.tensor_scalar_mul(
            out=top_over_beta[:], in0=top_bank[0:ROWS, 0, :], scalar1=neg_inv_beta[0:ROWS, 0:1]
        )
        sum_bank = psum.tile([P, PACK, P], F32, name="bank")
        nc.tensor.transpose(sum_bank[:, 0, :], exp_sums[:], ident[:])
        ln_sums = keep.tile([ROWS, P], F32)
        nc.scalar.activation(out=ln_sums[:], in_=sum_bank[0:ROWS, 0, :], func=ACT.Ln)
        out_rows = keep.tile([ROWS, P], F32)
        nc.vector.scalar_tensor_tensor(
            out=out_rows[:],
            in0=ln_sums[:],
            scalar=neg_inv_beta[0:ROWS, 0:1],
            in1=top_over_beta[:],
            op0=ALU.mult,
            op1=ALU.subtract,
        )
        nc.sync.dma_start(out=out.rearrange("b h (t p) -> (b h t) p", p=P), in_=out_rows[:])
